import numpy as np
import ml_dtypes

BF16 = ml_dtypes.bfloat16


def bf(x):
    return np.asarray(x, np.float32).astype(BF16)


def f32(x):
    return np.asarray(x, np.float32)


def f64(x):
    return np.asarray(x).astype(np.float64)


def striped(idx):
    return np.tile(idx.reshape(-1, 16).T, (8, 1))


C, S, N = 256, 1024, 256


def setup_inputs():
    return {"p_tab": f32(2.0 * np.random.standard_normal((C, S))), "logit": f32(1.5 * np.random.standard_normal((1, N))), "u_emb": f32(0.3 + 0.4 * np.random.standard_normal((C, 1))), "offs": striped(np.random.permutation(S)[:N])}


def reference(p_tab, logit, u_emb, offs):
    idx = offs[:16].T.reshape(-1)
    e = np.exp(f64(logit))
    a = e / e.sum(axis=1, keepdims=True)
    pooled = (f64(p_tab)[:, idx] * a).sum(axis=1, keepdims=True)
    return f64(u_emb) + pooled

@@ -1,0 +1,64 @@
+import concourse.mybir as mybir
+from concourse.masks import make_identity
+
+F32 = mybir.dt.float32
+U16 = mybir.dt.uint16
+MULT = mybir.AluOpType.mult
+ADD = mybir.AluOpType.add
+EXP = mybir.ActivationFunctionType.Exp
+X = mybir.AxisListType.X
+
+P = 128
+
+
+def tile_acfmodel_kernel(tc, p_tab, logit, u_emb, offs, out):
+    nc = tc.nc
+    C, S = p_tab.shape
+    N = logit.shape[1]
+    B = C // P
+
+    table_blocks = p_tab.rearrange("(b p) s -> b p s", p=P)
+    u_rows = u_emb.rearrange("(b p) o -> b (p o)", p=P)
+    out_rows = out.rearrange("(b p) o -> b (p o)", p=P)
+
+    with (
+        tc.tile_pool(name="held", bufs=1) as held,
+        tc.psum_pool(name="psum", bufs=1) as psum,
+    ):
+        offsets = held.tile([P, N // 16], U16, name="offsets")
+        nc.sync.dma_start(offsets[:], offs)
+
+        scores = held.tile([P, N], F32, name="scores")
+        nc.scalar.dma_start(scores[:], logit.broadcast_to([P, N]))
+
+        tables = [held.tile([P, S], F32, name=f"table{b}") for b in range(B)]
+        for b in range(B):
+            nc.sync.dma_start(tables[b][:], table_blocks[b])
+
+        user = held.tile([B, P], F32, name="user")
+        nc.scalar.dma_start(user[:], u_rows)
+
+        identity = held.tile([P, P], F32, name="identity")
+        make_identity(nc, identity[:])
+
+        neg_max = held.tile([P, 1], F32, name="neg_max")
+        nc.vector.reduce_max(neg_max[:], scores[:], X, negate=True)
+        expd = held.tile([P, N], F32, name="expd")
+        exp_sum = held.tile([P, 1], F32, name="exp_sum")
+        nc.scalar.activation(expd[:], scores[:], EXP, bias=neg_max[:], scale=1.0, accum_out=exp_sum[:])
+        inv_sum = held.tile([P, 1], F32, name="inv_sum")
+        nc.vector.reciprocal(inv_sum[:], exp_sum[:])
+        weights = held.tile([P, N], F32, name="weights")
+        nc.vector.tensor_scalar_mul(weights[:], expd[:], inv_sum[:])
+
+        pooled = held.tile([P, B], F32, name="pooled")
+        for b in range(B):
+            weighted = held.tile([P, N], F32, name=f"weighted{b}")
+            nc.vector.tensor_tensor(weighted[:], tables[b][:].indirect(offsets[:]), weights[:], MULT)
+            nc.vector.reduce_sum(pooled[:, b : b + 1], weighted[:], X)
+
+        pooled_rows = psum.tile([B, P], F32, name="pooled_rows")
+        nc.tensor.transpose(pooled_rows[:], pooled[:], identity[:])
+        result = held.tile([B, P], F32, name="result")
+        nc.vector.tensor_tensor(result[:], pooled_rows[:], user[:], ADD)
+        nc.sync.dma_start(out_rows, result[:])

@@ -41,6 +41,10 @@ def tile_acfmodel_kernel(tc, p_tab, logit, u_emb, offs, out):
         identity = held.tile([P, P], F32, name="identity")
         make_identity(nc, identity[:])
 
+        warm = held.tile([P, 1], F32, name="warm")
+        nc.vector.memset(warm[:], 0.0)
+        nc.scalar.activation(warm[:], warm[:], EXP)
+
         neg_max = held.tile([P, 1], F32, name="neg_max")
         nc.vector.reduce_max(neg_max[:], scores[:], X, negate=True)
         expd = held.tile([P, N], F32, name="expd")
@@ -48,17 +52,15 @@ def tile_acfmodel_kernel(tc, p_tab, logit, u_emb, offs, out):
         nc.scalar.activation(expd[:], scores[:], EXP, bias=neg_max[:], scale=1.0, accum_out=exp_sum[:])
         inv_sum = held.tile([P, 1], F32, name="inv_sum")
         nc.vector.reciprocal(inv_sum[:], exp_sum[:])
-        weights = held.tile([P, N], F32, name="weights")
-        nc.vector.tensor_scalar_mul(weights[:], expd[:], inv_sum[:])
 
         pooled = held.tile([P, B], F32, name="pooled")
         for b in range(B):
             weighted = held.tile([P, N], F32, name=f"weighted{b}")
-            nc.vector.tensor_tensor(weighted[:], tables[b][:].indirect(offsets[:]), weights[:], MULT)
+            nc.vector.tensor_tensor(weighted[:], tables[b][:].indirect(offsets[:]), expd[:], MULT)
             nc.vector.reduce_sum(pooled[:, b : b + 1], weighted[:], X)
 
         pooled_rows = psum.tile([B, P], F32, name="pooled_rows")
         nc.tensor.transpose(pooled_rows[:], pooled[:], identity[:])
         result = held.tile([B, P], F32, name="result")
-        nc.vector.tensor_tensor(result[:], pooled_rows[:], user[:], ADD)
+        nc.vector.scalar_tensor_tensor(result[:], pooled_rows[:], inv_sum[0:B, :], user[:], MULT, ADD)
         nc.sync.dma_start(out_rows, result[:])

@@ -57,10 +57,12 @@ def tile_acfmodel_kernel(tc, p_tab, logit, u_emb, offs, out):
         for b in range(B):
             weighted = held.tile([P, N], F32, name=f"weighted{b}")
             nc.vector.tensor_tensor(weighted[:], tables[b][:].indirect(offsets[:]), expd[:], MULT)
-            nc.vector.reduce_sum(pooled[:, b : b + 1], weighted[:], X)
+            nc.vector.tensor_scalar(
+                weighted[:], weighted[:], inv_sum[:], None, MULT, ADD, accum_out=pooled[:, b : b + 1]
+            )
 
         pooled_rows = psum.tile([B, P], F32, name="pooled_rows")
         nc.tensor.transpose(pooled_rows[:], pooled[:], identity[:])
         result = held.tile([B, P], F32, name="result")
-        nc.vector.scalar_tensor_tensor(result[:], pooled_rows[:], inv_sum[0:B, :], user[:], MULT, ADD)
+        nc.vector.tensor_tensor(result[:], pooled_rows[:], user[:], ADD)
         nc.sync.dma_start(out_rows, result[:])

@@ -1,5 +1,4 @@
 import concourse.mybir as mybir
-from concourse.masks import make_identity
 
 F32 = mybir.dt.float32
 U16 = mybir.dt.uint16
@@ -9,6 +8,7 @@ EXP = mybir.ActivationFunctionType.Exp
 X = mybir.AxisListType.X
 
 P = 128
+T = 32
 
 
 def tile_acfmodel_kernel(tc, p_tab, logit, u_emb, offs, out):
@@ -18,13 +18,10 @@ def tile_acfmodel_kernel(tc, p_tab, logit, u_emb, offs, out):
     B = C // P
 
     table_blocks = p_tab.rearrange("(b p) s -> b p s", p=P)
-    u_rows = u_emb.rearrange("(b p) o -> b (p o)", p=P)
-    out_rows = out.rearrange("(b p) o -> b (p o)", p=P)
+    u_runs = u_emb.rearrange("(b q t) o -> b q (t o)", b=B, t=T)
+    out_runs = out.rearrange("(b q t) o -> b q (t o)", b=B, t=T)
 
-    with (
-        tc.tile_pool(name="held", bufs=1) as held,
-        tc.psum_pool(name="psum", bufs=1) as psum,
-    ):
+    with tc.tile_pool(name="held", bufs=1) as held:
         offsets = held.tile([P, N // 16], U16, name="offsets")
         nc.sync.dma_start(offsets[:], offs)
 
@@ -35,11 +32,12 @@ def tile_acfmodel_kernel(tc, p_tab, logit, u_emb, offs, out):
         for b in range(B):
             nc.sync.dma_start(tables[b][:], table_blocks[b])
 
-        user = held.tile([B, P], F32, name="user")
-        nc.scalar.dma_start(user[:], u_rows)
-
-        identity = held.tile([P, P], F32, name="identity")
-        make_identity(nc, identity[:])
+        user_runs = held.tile([P, T], F32, name="user_runs", align_bytes=64)
+        nc.vector.memset(user_runs[:], 0.0)
+        for b in range(B):
+            nc.scalar.dma_start(user_runs[b::T, :], u_runs[b])
+        user_cols = held.tile([P, T], F32, name="user_cols", align_bytes=64)
+        nc.vector.transpose(user_cols[:], user_runs[:])
 
         warm = held.tile([P, 1], F32, name="warm")
         nc.vector.memset(warm[:], 0.0)
@@ -53,16 +51,23 @@ def tile_acfmodel_kernel(tc, p_tab, logit, u_emb, offs, out):
         inv_sum = held.tile([P, 1], F32, name="inv_sum")
         nc.vector.reciprocal(inv_sum[:], exp_sum[:])
 
-        pooled = held.tile([P, B], F32, name="pooled")
+        result_cols = held.tile([P, T], F32, name="result_cols", align_bytes=64)
+        nc.vector.memset(result_cols[:], 0.0)
         for b in range(B):
             weighted = held.tile([P, N], F32, name=f"weighted{b}")
             nc.vector.tensor_tensor(weighted[:], tables[b][:].indirect(offsets[:]), expd[:], MULT)
             nc.vector.tensor_scalar(
-                weighted[:], weighted[:], inv_sum[:], None, MULT, ADD, accum_out=pooled[:, b : b + 1]
+                weighted[:],
+                weighted[:],
+                inv_sum[:],
+                user_cols[:, b : b + 1],
+                MULT,
+                ADD,
+                accum_out=result_cols[:, b : b + 1],
             )
 
-        pooled_rows = psum.tile([B, P], F32, name="pooled_rows")
-        nc.tensor.transpose(pooled_rows[:], pooled[:], identity[:])
-        result = held.tile([B, P], F32, name="result")
-        nc.vector.tensor_tensor(result[:], pooled_rows[:], user[:], ADD)
-        nc.sync.dma_start(out_rows, result[:])
+        result_runs = held.tile([P, T], F32, name="result_runs", align_bytes=64)
+        nc.vector.transpose(result_runs[:], result_cols[:])
+        store_queues = [nc.sync, nc.scalar]
+        for b in range(B):
+            store_queues[b % 2].dma_start(out_runs[b], result_runs[b::T, :])

@@ -18,7 +18,7 @@ def tile_acfmodel_kernel(tc, p_tab, logit, u_emb, offs, out):
     B = C // P
 
     table_blocks = p_tab.rearrange("(b p) s -> b p s", p=P)
-    u_runs = u_emb.rearrange("(b q t) o -> b q (t o)", b=B, t=T)
+    u_blocks = u_emb.rearrange("(b p) o -> b p o", p=P)
     out_runs = out.rearrange("(b q t) o -> b q (t o)", b=B, t=T)
 
     with tc.tile_pool(name="held", bufs=1) as held:
@@ -32,12 +32,9 @@ def tile_acfmodel_kernel(tc, p_tab, logit, u_emb, offs, out):
         for b in range(B):
             nc.sync.dma_start(tables[b][:], table_blocks[b])
 
-        user_runs = held.tile([P, T], F32, name="user_runs", align_bytes=64)
-        nc.vector.memset(user_runs[:], 0.0)
+        users = [held.tile([P, 1], F32, name=f"user{b}") for b in range(B)]
         for b in range(B):
-            nc.scalar.dma_start(user_runs[b::T, :], u_runs[b])
-        user_cols = held.tile([P, T], F32, name="user_cols", align_bytes=64)
-        nc.vector.transpose(user_cols[:], user_runs[:])
+            nc.scalar.dma_start(users[b][:], u_blocks[b])
 
         warm = held.tile([P, 1], F32, name="warm")
         nc.vector.memset(warm[:], 0.0)
@@ -60,7 +57,7 @@ def tile_acfmodel_kernel(tc, p_tab, logit, u_emb, offs, out):
                 weighted[:],
                 weighted[:],
                 inv_sum[:],
-                user_cols[:, b : b + 1],
+                users[b][:],
                 MULT,
                 ADD,
                 accum_out=result_cols[:, b : b + 1],

@@ -18,7 +18,7 @@ def tile_acfmodel_kernel(tc, p_tab, logit, u_emb, offs, out):
     B = C // P
 
     table_blocks = p_tab.rearrange("(b p) s -> b p s", p=P)
-    u_blocks = u_emb.rearrange("(b p) o -> b p o", p=P)
+    u_runs = u_emb.rearrange("(b q t) o -> b q (t o)", b=B, t=T)
     out_runs = out.rearrange("(b q t) o -> b q (t o)", b=B, t=T)
 
     with tc.tile_pool(name="held", bufs=1) as held:
@@ -29,12 +29,15 @@ def tile_acfmodel_kernel(tc, p_tab, logit, u_emb, offs, out):
         nc.scalar.dma_start(scores[:], logit.broadcast_to([P, N]))
 
         tables = [held.tile([P, S], F32, name=f"table{b}") for b in range(B)]
-        for b in range(B):
-            nc.sync.dma_start(tables[b][:], table_blocks[b])
+        nc.sync.dma_start(tables[0][:], table_blocks[0])
 
-        users = [held.tile([P, 1], F32, name=f"user{b}") for b in range(B)]
+        user_runs = held.tile([P, T], F32, name="user_runs", align_bytes=64)
+        nc.gpsimd.memset(user_runs[:], 0.0)
         for b in range(B):
-            nc.scalar.dma_start(users[b][:], u_blocks[b])
+            nc.scalar.dma_start(user_runs[b::T, :], u_runs[b])
+        nc.scalar.dma_start(tables[1][:], table_blocks[1])
+        user_cols = held.tile([P, T], F32, name="user_cols", align_bytes=64)
+        nc.vector.transpose(user_cols[:], user_runs[:])
 
         warm = held.tile([P, 1], F32, name="warm")
         nc.vector.memset(warm[:], 0.0)
@@ -57,7 +60,7 @@ def tile_acfmodel_kernel(tc, p_tab, logit, u_emb, offs, out):
                 weighted[:],
                 weighted[:],
                 inv_sum[:],
-                users[b][:],
+                user_cols[:, b : b + 1],
                 MULT,
                 ADD,
                 accum_out=result_cols[:, b : b + 1],

@@ -51,9 +51,10 @@ def tile_acfmodel_kernel(tc, p_tab, logit, u_emb, offs, out):
         inv_sum = held.tile([P, 1], F32, name="inv_sum")
         nc.vector.reciprocal(inv_sum[:], exp_sum[:])
 
-        result_cols = held.tile([P, T], F32, name="result_cols", align_bytes=64)
-        nc.vector.memset(result_cols[:], 0.0)
+        store_queues = [nc.scalar, nc.sync]
         for b in range(B):
+            result_cols = held.tile([P, T], F32, name=f"result_cols{b}", align_bytes=64)
+            nc.vector.memset(result_cols[:], 0.0)
             weighted = held.tile([P, N], F32, name=f"weighted{b}")
             nc.vector.tensor_tensor(weighted[:], tables[b][:].indirect(offsets[:]), expd[:], MULT)
             nc.vector.tensor_scalar(
@@ -63,11 +64,8 @@ def tile_acfmodel_kernel(tc, p_tab, logit, u_emb, offs, out):
                 user_cols[:, b : b + 1],
                 MULT,
                 ADD,
-                accum_out=result_cols[:, b : b + 1],
+                accum_out=result_cols[:, 0:1],
             )
-
-        result_runs = held.tile([P, T], F32, name="result_runs", align_bytes=64)
-        nc.vector.transpose(result_runs[:], result_cols[:])
-        store_queues = [nc.sync, nc.scalar]
-        for b in range(B):
-            store_queues[b % 2].dma_start(out_runs[b], result_runs[b::T, :])
+            result_runs = held.tile([P, T], F32, name=f"result_runs{b}", align_bytes=64)
+            nc.vector.transpose(result_runs[:], result_cols[:])
+            store_queues[b].dma_start(out_runs[b], result_runs[::T, :])

import concourse.mybir as mybir

F32 = mybir.dt.float32
U16 = mybir.dt.uint16
MULT = mybir.AluOpType.mult
ADD = mybir.AluOpType.add
EXP = mybir.ActivationFunctionType.Exp
X = mybir.AxisListType.X

P = 128
T = 32


def tile_acfmodel_kernel(tc, p_tab, logit, u_emb, offs, out):
    nc = tc.nc
    C, S = p_tab.shape
    N = logit.shape[1]
    B = C // P

    table_blocks = p_tab.rearrange("(b p) s -> b p s", p=P)
    u_runs = u_emb.rearrange("(b q t) o -> b q (t o)", b=B, t=T)
    out_runs = out.rearrange("(b q t) o -> b q (t o)", b=B, t=T)

    with tc.tile_pool(name="held", bufs=1) as held:
        offsets = held.tile([P, N // 16], U16, name="offsets")
        nc.sync.dma_start(offsets[:], offs)

        scores = held.tile([P, N], F32, name="scores")
        nc.scalar.dma_start(scores[:], logit.broadcast_to([P, N]))

        tables = [held.tile([P, S], F32, name=f"table{b}") for b in range(B)]
        nc.sync.dma_start(tables[0][:], table_blocks[0])

        user_runs = held.tile([P, T], F32, name="user_runs", align_bytes=64)
        nc.gpsimd.memset(user_runs[:], 0.0)
        for b in range(B):
            nc.scalar.dma_start(user_runs[b::T, :], u_runs[b])
        nc.scalar.dma_start(tables[1][:], table_blocks[1])
        user_cols = held.tile([P, T], F32, name="user_cols", align_bytes=64)
        nc.vector.transpose(user_cols[:], user_runs[:])

        warm = held.tile([P, 1], F32, name="warm")
        nc.vector.memset(warm[:], 0.0)
        nc.scalar.activation(warm[:], warm[:], EXP)

        neg_max = held.tile([P, 1], F32, name="neg_max")
        nc.vector.reduce_max(neg_max[:], scores[:], X, negate=True)
        expd = held.tile([P, N], F32, name="expd")
        exp_sum = held.tile([P, 1], F32, name="exp_sum")
        nc.scalar.activation(expd[:], scores[:], EXP, bias=neg_max[:], scale=1.0, accum_out=exp_sum[:])
        inv_sum = held.tile([P, 1], F32, name="inv_sum")
        nc.vector.reciprocal(inv_sum[:], exp_sum[:])

        store_queues = [nc.scalar, nc.sync]
        for b in range(B):
            result_cols = held.tile([P, T], F32, name=f"result_cols{b}", align_bytes=64)
            nc.vector.memset(result_cols[:], 0.0)
            weighted = held.tile([P, N], F32, name=f"weighted{b}")
            nc.vector.tensor_tensor(weighted[:], tables[b][:].indirect(offsets[:]), expd[:], MULT)
            nc.vector.tensor_scalar(
                weighted[:],
                weighted[:],
                inv_sum[:],
                user_cols[:, b : b + 1],
                MULT,
                ADD,
                accum_out=result_cols[:, 0:1],
            )
            result_runs = held.tile([P, T], F32, name=f"result_runs{b}", align_bytes=64)
            nc.vector.transpose(result_runs[:], result_cols[:])
            store_queues[b].dma_start(out_runs[b], result_runs[::T, :])
